import numpy as np
import ml_dtypes


def mxq(x, axis, fmt="e4m3"):
    dtype, down = {"e4m3": (ml_dtypes.float8_e4m3fn, 7), "e5m2": (ml_dtypes.float8_e5m2, 14)}[fmt]
    v = np.moveaxis(np.asarray(x, np.float32).astype(ml_dtypes.bfloat16).astype(np.float64), axis, -1)
    blocks = v.reshape(v.shape[:-1] + (-1, 32))
    amax = np.abs(blocks).max(-1, keepdims=True)
    byte = np.maximum(np.where(amax > 0, np.frexp(amax)[1] - 1 + 127, 0) - down, 1)
    scale = np.exp2(byte - 127.0)
    codes = (blocks / scale).astype(np.float32).astype(dtype).astype(np.float64)
    return np.moveaxis((codes * scale).reshape(v.shape), -1, axis)


WIDE = False


def mx_kscale(k):
    if not WIDE:
        return np.ones(k)
    levels = np.array([18, -18])
    if k % 512:
        return np.exp2(np.random.permutation(np.resize(levels, k // 32))).repeat(32)
    a = np.empty((k // 512, 16))
    for p in range(k // 512):
        a[p, :8] = np.random.permutation(np.resize(levels, 8))
        for g in range(8):
            far = levels[np.abs(levels - a[p, g]) >= 10]
            a[p, g + 8] = far[np.random.randint(len(far))]
    return np.exp2(a.ravel()).repeat(32)


BF16 = ml_dtypes.bfloat16


def bf(x):
    return np.asarray(x, np.float32).astype(BF16)


def f64(x):
    return np.asarray(x).astype(np.float64)


B, N, IN_DIM, OUT_DIM, H = 1, 1024, 512, 1024, 2
HEAD_DIM = OUT_DIM // H
EDGE_P = 0.01


def split_heads(y):
    return y.reshape(B, N, H, HEAD_DIM).transpose(0, 2, 1, 3)


def setup_inputs():
    s = mx_kscale(N)
    t = mx_kscale(N)
    u = mx_kscale(OUT_DIM)
    adj0 = bf(np.maximum((np.random.random((N, N)) < EDGE_P) * 1.0, np.eye(N)))
    q = bf(np.random.standard_normal((B, H, N, HEAD_DIM)))
    k = bf(np.random.standard_normal((B, H, N, HEAD_DIM)))
    h0 = bf(np.random.standard_normal((B, N, IN_DIM)))
    w0 = bf(np.random.standard_normal((IN_DIM, OUT_DIM)) / np.sqrt(IN_DIM))
    g = bf(4.0 * np.random.standard_normal((B, N, OUT_DIM)) * np.exp2(np.random.randint(-6, 1, (B, N, 1))) / s[:, None] * u)
    scores = f64(q) @ f64(k).transpose(0, 1, 3, 2) / np.sqrt(HEAD_DIM)
    lse = np.log((f64(adj0) * np.exp(scores)).sum(-1))
    return {"q": q, "k": k,
            "h": bf(f64(h0) / t[:, None]),
            "w_v": bf(f64(w0) / u),
            "adj": bf(f64(adj0) * s[:, None] * t),
            "scores": np.asarray(scores, np.float32),
            "lse": np.asarray(lse, np.float32),
            "grad_out": g}


def reference(q, k, h, w_v, adj, scores, lse, grad_out):
    p = f64(adj) * np.exp(f64(scores) - f64(lse)[..., None])
    g = split_heads(f64(grad_out))
    dv = mxq(p, 2, "e4m3").transpose(0, 1, 3, 2) @ mxq(g, 2, "e5m2")
    dz1 = dv.transpose(0, 2, 1, 3).reshape(B * N, OUT_DIM)
    dh = mxq(dz1, 1, "e5m2") @ mxq(f64(w_v), 1, "e4m3").T
    dw = mxq(f64(h).reshape(B * N, IN_DIM), 0, "e4m3").T @ mxq(dz1, 0, "e5m2")
    return dh.reshape(B, N, IN_DIM), dw

@@ -1,0 +1,253 @@
+from contextlib import ExitStack
+
+import concourse.mybir as mybir
+from concourse.masks import make_identity
+
+F32 = mybir.dt.float32
+BF16 = mybir.dt.bfloat16
+U32 = mybir.dt.uint32
+U8 = mybir.dt.uint8
+E4M3 = mybir.dt.float8_e4m3fn_x4
+E5M2 = mybir.dt.float8_e5m2_x4
+EXP = mybir.ActivationFunctionType.Exp
+MULT = mybir.AluOpType.mult
+
+FLOPS = 2 * 1024 * 1024 * 1024 * 2
+BYTES = 18890752
+
+P = 128
+LOADS = """g10 g01 g00 sc0010 sc0011 adj01 sc1000 sc1001 adj00 sc0000 sc0001 g11 sc1010 adj11 sc1011 sc1110 sc1111 sc1100 sc1101 adj10 sc0100 w sc0101 sc0110 h0 sc0111 h1"""
+ORDER = """Gc10:V Gc01:S Qg10:V E0010:S E0011:S Qg01:V Gc00:V E0012:S E0013:S M0010:V E1000:S E1001:S Qg00:V M0011:V E1002:S
+E1003:S M1000:V E0000:S E0001:S M1001:V E0002:S E0003:S Qp0010:V Qp1000:V Gc11:S M0001:V DF103:0 DF100:1 DF101:2
+M0000:V E1010:S E1011:S Qp0000:V Qg11:V DF000:3 E1012:S E1013:S D000:P DF102:4 C000:V DF001:5 E1110:S E1111:S DF003:6
+M1010:V DF002:7 D001:P D003:P E1112:S E1113:S D002:P M1011:V E1100:S E1101:S M1111:V E1102:S E1103:S Qp1010:V M1110:V
+C001:S C003:S T000:3 M1101:V C002:S D100:P D101:P E0100:S E0101:S A001:V D102:P D103:P M1100:V C102:S W01:5 C103:S
+W00:6 Qp1111:V Wc01:S Qp1100:V T001:7 E0102:S E0103:S A000:V DF111:4 T101:0 C100:V C101:S Qp1110:V DF110:5 E0110:S
+E0111:S DF112:1 M0101:V D112:P T100:2 Wc00:S M0100:V B100:S DF113:6 C112:S W11:2 Qw0:V E0112:S E0113:S Qp0100:V
+D111:P Qa00:V DF010:1 B101:S D113:P M0110:V C111:S DF012:0 D110:P C113:S W10:4 M0111:V C110:S T111:6 Wc11:S Qb10:V
+DF013:5 Wc10:S T110:2 Hc0:V B001:S DF011:4 B000:S OF02:7 B110:S Qp0110:V OF00:3 A101:S A100:V D013:P OF03:2 D011:P
+Qh0:V D012:P B111:S D010:P Qw1:V C013:S OF01:6 Qa10:V C012:S Qb00:V O00:P C011:S T011:5 C010:V Hc1:S Oc00:V PF01:0
+T010:4 B011:V So00:L O01:P A011:V PF12:1 O03:P Qb11:V O02:P B010:S PF11:3 Qh1:V PF13:5 Oc02:S PF10:4 A010:V P13:P
+Oc03:S So02:L PF03:7 P10:P Qb01:V Oc01:S So03:L P12:P PF02:2 A110:V Pc13:S So01:L P03:P PF00:6 Pc10:S A111:V Sp13:L
+P01:P P11:P Pc12:S Sp10:L P02:P Qa01:V P00:P Pc11:S Sp12:L Qa11:V OF11:5 Pc03:S Sp11:L OF12:4 O11:P Pc02:S Sp03:L
+O12:P OF10:1 Oc11:S Sp02:L OF13:3 O10:P Oc12:S So11:L O13:P Pc00:S So12:L Oc10:S Sp00:L Oc13:S So10:L Pc01:S So13:L
+Sp01:L"""
+
+
+def tile_gatlayer_pa_v_kernel(tc, q, k, h, w_v, adj, scores, lse, grad_out, out_0, out_1):
+    nc = tc.nc
+    with ExitStack() as ctx:
+        pool = ctx.enter_context(tc.tile_pool(name="sb", bufs=1))
+        psum = ctx.enter_context(tc.psum_pool(name="ps", bufs=1))
+
+        scores_v = scores[0].rearrange("n (g p s) j -> n g p s j", p=P, s=4)
+        adj_v = adj.rearrange("(g p s) j -> g p s j", p=P, s=4)
+        g_v = grad_out[0].rearrange("(g p s) f -> g p s f", p=P, s=4)
+        h_v = h[0].rearrange("(g p s) c -> g p s c", p=P, s=4)
+        w_vv = w_v.rearrange("(a p) f -> p a f", p=P)
+        out0_v = out_0[0].rearrange("(a p) c -> a p c", p=P)
+        out1_v = out_1.rearrange("(a p) f -> a p f", p=P)
+
+        T = {}
+
+        def sb(key, shape, dt, tag, bufs):
+            T[key] = pool.tile(shape, dt, name=tag, tag=tag, bufs=bufs, align_bytes=64)
+            return T[key]
+
+        def grouped(key, tag, bufs):
+            return sb(key, [P, 512, 4], BF16, tag, bufs)
+
+        def codes(key, tag, bufs):
+            sb("c" + key, [P, 512], U32, "c" + tag, bufs)
+            sb("s" + key, [P, 512], U8, "s" + tag, bufs)
+
+        def quant(key, src, fmt, lo=0, hi=512):
+            nc.vector.quantize_mx(
+                out=T["c" + key][:, lo:hi].bitcast(fmt),
+                scales=T["s" + key][:, lo:hi],
+                in_=T[src][:, lo:hi, :].rearrange("p c t -> p (c t)"),
+            )
+
+        def mm(bank, lk, lf, cols, rk, rf, start, stop):
+            nc.tensor.matmul_mx(
+                out=bank[:],
+                lhsT=T["c" + lk][:, cols].bitcast(lf),
+                lhsT_scale=T["s" + lk][:, cols],
+                rhs=T["c" + rk][:].bitcast(rf),
+                rhs_scale=T["s" + rk][:],
+                start=start,
+                stop=stop,
+            )
+
+        def copy(eng, out, in_):
+            if eng == "V":
+                nc.vector.tensor_copy(out=out, in_=in_)
+            else:
+                nc.scalar.copy(out=out, in_=in_)
+
+        def bank(key, b):
+            T[key] = psum.tile([P, 512], F32, name="bank%d" % b, tag="bank%d" % b, bufs=1)
+            return T[key]
+
+        def blk(j):
+            return slice(128 * j, 128 * j + 128)
+
+        with tc.manual_schedule():
+            dummy = pool.tile([P, 1], F32, name="dummy", tag="dummy")
+            nc.vector.memset(dummy[:], 0.0)
+            warm = pool.tile([P, 1], F32, name="warm", tag="warm")
+            nc.scalar.activation(warm[:], dummy[:], EXP)
+            ident = pool.tile([P, P], F32, name="ident", tag="ident")
+            make_identity(nc, ident[:])
+            lse_sb = pool.tile([P, 4, 4], F32, name="lse_sb", tag="lse_sb")
+            nlse = pool.tile([P, 4, 4], F32, name="nlse", tag="nlse")
+            nc.scalar.dma_start(out=lse_sb[:], in_=lse.rearrange("b n i -> (b n i)").rearrange("(q p s) -> p q s", p=P, s=4))
+
+            for ld in LOADS.split():
+                if ld[:2] == "sc":
+                    n, G, g, hf = [int(x) for x in ld[2:]]
+                    key = "sc%d%d%d" % (n, G, g)
+                    if hf == 0:
+                        sb(key, [P, 4, 512], F32, "sc", 5)
+                    nc.sync.dma_start(out=T[key][:, 2 * hf : 2 * hf + 2, :], in_=scores_v[n, g][:, 2 * hf : 2 * hf + 2, 512 * G : 512 * G + 512])
+                elif ld[:3] == "adj":
+                    G, g = int(ld[3]), int(ld[4])
+                    sb(ld, [P, 4, 512], BF16, "adj", 4)
+                    nc.sync.dma_start(out=T[ld][:], in_=adj_v[g][:, :, 512 * G : 512 * G + 512])
+                elif ld[0] == "g":
+                    n, g = int(ld[1]), int(ld[2])
+                    sb(ld, [P, 4, 512], BF16, "raw", 4)
+                    nc.sync.dma_start(out=T[ld][:], in_=g_v[g][:, :, 512 * n : 512 * n + 512])
+                elif ld[0] == "h":
+                    sb(ld, [P, 4, 512], BF16, "raw", 4)
+                    nc.sync.dma_start(out=T[ld][:], in_=h_v[int(ld[1])])
+                elif ld == "w":
+                    sb(ld, [P, 4, 1024], BF16, "w", 1)
+                    nc.sync.dma_start(out=T[ld][:], in_=w_vv)
+            nc.vector.tensor_scalar(out=nlse[:], in0=lse_sb[:], scalar1=-1.0, scalar2=None, op0=MULT)
+
+            def transposes(src, col0, kk, bk):
+                for i in range(2):
+                    words = T[src][:, 2 * kk + i, :].bitcast(F32)
+                    for u in range(2):
+                        nc.tensor.transpose(bk[:, 128 * (2 * i + u) : 128 * (2 * i + u) + 128], words[:, col0 + u : col0 + 256 : 2], ident[:])
+
+            def words_out(eng, dst, kk, bk):
+                copy(
+                    eng,
+                    T[dst][:].rearrange("p c t -> p (c t)").bitcast(F32)[:, 512 * kk : 512 * kk + 512].rearrange("p (i r u) -> p i r u", i=2, u=2),
+                    bk[:].rearrange("p (i u r) -> p i r u", i=2, u=2),
+                )
+
+            for item in ORDER.split():
+                nm, e = item.split(":")
+                kind = nm
+                for dg in "0123456789":
+                    kind = kind.replace(dg, "")
+                d = [int(x) for x in nm[len(kind) :]]
+                if kind == "E":
+                    n, G, g, s = d
+                    key = "e%d%d%d" % (n, G, g)
+                    if key not in T:
+                        sb(key, [P, 4, 512], F32, "e", 3)
+                    nc.scalar.activation(T[key][:, s, :], T["sc%d%d%d" % (n, G, g)][:, s, :], EXP, bias=nlse[:, 2 * n + g, s : s + 1])
+                elif kind == "M":
+                    n, G, g, hh = d
+                    key = "p%d%d%d" % (n, G, g)
+                    if key not in T:
+                        grouped(key, "gp", 3)
+                    c = slice(256 * hh, 256 * hh + 256)
+                    nc.vector.tensor_tensor(
+                        out=T[key][:, c, :].rearrange("p (c i) s -> p c s i", i=4),
+                        in0=T["e%d%d%d" % (n, G, g)][:, :, c].rearrange("p s (c i) -> p c s i", i=4),
+                        in1=T["adj%d%d" % (G, g)][:, :, c].rearrange("p s (c i) -> p c s i", i=4),
+                        op=MULT,
+                    )
+                elif kind == "Qp":
+                    n, G, g, hh = d
+                    key = "p%d%d%d" % (n, G, g)
+                    if "c" + key not in T:
+                        codes(key, "p", 6)
+                    if (n, G, g) == (1, 1, 1):
+                        quant(key, key, E4M3, 256 * hh, 256 * hh + 256)
+                    else:
+                        quant(key, key, E4M3)
+                elif kind == "Gc":
+                    n, g = d
+                    grouped("gg%d%d" % (n, g), "gg", 3)
+                    copy(e, T["gg%d%d" % (n, g)][:].rearrange("p (t m) s -> p t m s", t=4), T["g%d%d" % (n, g)][:].rearrange("p s (m t) -> p t m s", t=4))
+                elif kind == "Qg":
+                    key = "gg%d%d" % (d[0], d[1])
+                    codes(key, "g", 4)
+                    quant(key, key, E5M2)
+                elif kind == "Hc":
+                    grouped("hh%d" % d[0], "hh", 1)
+                    copy(e, T["hh%d" % d[0]][:].rearrange("p (c i) s -> p c s i", i=4), T["h%d" % d[0]][:].rearrange("p s (c i) -> p c s i", i=4))
+                elif kind == "Qh":
+                    key = "hh%d" % d[0]
+                    codes(key, "h", 2)
+                    quant(key, key, E4M3)
+                elif kind == "W":
+                    transposes("w", 256 * d[0], d[1], bank(nm, int(e)))
+                elif kind == "Wc":
+                    key = "ww%d" % d[0]
+                    if key not in T:
+                        grouped(key, "ww", 1)
+                    words_out(e, key, d[1], T["W%d%d" % (d[0], d[1])])
+                elif kind == "Qw":
+                    key = "ww%d" % d[0]
+                    codes(key, "w", 2)
+                    quant(key, key, E4M3)
+                elif kind == "DF":
+                    n, G, t = d
+                    mm(bank("D%d%d%d" % (n, G, t), int(e)), "gg%d0" % n, E5M2, blk(t), "p%d%d0" % (n, G), E4M3, True, False)
+                elif kind == "D":
+                    n, G, t = d
+                    mm(T[nm], "gg%d1" % n, E5M2, blk(t), "p%d%d1" % (n, G), E4M3, False, True)
+                elif kind == "C":
+                    n, G, t = d
+                    key = "v%d%d" % (n, G)
+                    if key not in T:
+                        sb(key, [P, 4, 512], BF16, "v", 2)
+                    copy(e, T[key][:, t, :], T["D%d%d%d" % (n, G, t)][:])
+                elif kind == "A":
+                    n, G, hh = d
+                    key = "a%d%d" % (n, G)
+                    if key not in T:
+                        grouped(key, "a", 2)
+                    c = slice(256 * hh, 256 * hh + 256)
+                    copy(e, T[key][:, c, :].rearrange("p (c i) t -> p c t i", i=4), T["v%d%d" % (n, G)][:, :, c].rearrange("p t (c i) -> p c t i", i=4))
+                elif kind == "Qa" or kind == "Qb":
+                    key = kind[1] + "%d%d" % (d[0], d[1])
+                    codes(key, kind[1], 4)
+                    quant(key, key, E5M2)
+                elif kind == "T":
+                    transposes("v%d%d" % (d[0], d[1]), 0, d[2], bank(nm, int(e)))
+                elif kind == "B":
+                    n, G, kk = d
+                    key = "b%d%d" % (n, G)
+                    if key not in T:
+                        grouped(key, "b", 2)
+                    words_out(e, key, kk, T["T%d%d%d" % (n, G, kk)])
+                elif kind == "OF":
+                    G, j = d
+                    mm(bank("O%d%d" % (G, j), int(e)), "a0%d" % G, E5M2, blk(j), "ww0", E4M3, True, False)
+                elif kind == "O":
+                    G, j = d
+                    mm(T[nm], "a1%d" % G, E5M2, blk(j), "ww1", E4M3, False, True)
+                elif kind == "PF":
+                    n, j = d
+                    mm(bank("P%d%d" % (n, j), int(e)), "hh0", E4M3, blk(j), "b%d0" % n, E5M2, True, False)
+                elif kind == "P":
+                    n, j = d
+                    mm(T[nm], "hh1", E4M3, blk(j), "b%d1" % n, E5M2, False, True)
+                elif kind == "Oc":
+                    o = sb("o" + nm, [P, 512], F32, "o", 6)
+                    copy(e, o[:], T["O%d%d" % (d[0], d[1])][:])
+                elif kind == "Pc":
+                    o = sb("o" + nm, [P, 512], F32, "o", 6)
+                    copy(e, o[:].rearrange("p (m t) -> p m t", t=4), T["P%d%d" % (d[0], d[1])][:].rearrange("p (t m) -> p m t", t=4))
+                elif kind == "So":
+                    nc.sync.dma_start(out=out0_v[4 * d[0] + d[1]], in_=T["oOc%d%d" % (d[0], d[1])][:])
+                elif kind == "Sp":
+                    nc.sync.dma_start(out=out1_v[d[1]][:, 512 * d[0] : 512 * d[0] + 512], in_=T["oPc%d%d" % (d[0], d[1])][:])

@@ -16,22 +16,22 @@ FLOPS = 2 * 1024 * 1024 * 1024 * 2
 BYTES = 18890752
 
 P = 128
-LOADS = """g10 g01 g00 sc0010 sc0011 adj01 sc1000 sc1001 adj00 sc0000 sc0001 g11 sc1010 adj11 sc1011 sc1110 sc1111 sc1100 sc1101 adj10 sc0100 w sc0101 sc0110 h0 sc0111 h1"""
-ORDER = """Gc10:V Gc01:S Qg10:V E0010:S E0011:S Qg01:V Gc00:V E0012:S E0013:S M0010:V E1000:S E1001:S Qg00:V M0011:V E1002:S
-E1003:S M1000:V E0000:S E0001:S M1001:V E0002:S E0003:S Qp0010:V Qp1000:V Gc11:S M0001:V DF103:0 DF100:1 DF101:2
-M0000:V E1010:S E1011:S Qp0000:V Qg11:V DF000:3 E1012:S E1013:S D000:P DF102:4 C000:V DF001:5 E1110:S E1111:S DF003:6
-M1010:V DF002:7 D001:P D003:P E1112:S E1113:S D002:P M1011:V E1100:S E1101:S M1111:V E1102:S E1103:S Qp1010:V M1110:V
-C001:S C003:S T000:3 M1101:V C002:S D100:P D101:P E0100:S E0101:S A001:V D102:P D103:P M1100:V C102:S W01:5 C103:S
-W00:6 Qp1111:V Wc01:S Qp1100:V T001:7 E0102:S E0103:S A000:V DF111:4 T101:0 C100:V C101:S Qp1110:V DF110:5 E0110:S
-E0111:S DF112:1 M0101:V D112:P T100:2 Wc00:S M0100:V B100:S DF113:6 C112:S W11:2 Qw0:V E0112:S E0113:S Qp0100:V
-D111:P Qa00:V DF010:1 B101:S D113:P M0110:V C111:S DF012:0 D110:P C113:S W10:4 M0111:V C110:S T111:6 Wc11:S Qb10:V
-DF013:5 Wc10:S T110:2 Hc0:V B001:S DF011:4 B000:S OF02:7 B110:S Qp0110:V OF00:3 A101:S A100:V D013:P OF03:2 D011:P
-Qh0:V D012:P B111:S D010:P Qw1:V C013:S OF01:6 Qa10:V C012:S Qb00:V O00:P C011:S T011:5 C010:V Hc1:S Oc00:V PF01:0
-T010:4 B011:V So00:L O01:P A011:V PF12:1 O03:P Qb11:V O02:P B010:S PF11:3 Qh1:V PF13:5 Oc02:S PF10:4 A010:V P13:P
-Oc03:S So02:L PF03:7 P10:P Qb01:V Oc01:S So03:L P12:P PF02:2 A110:V Pc13:S So01:L P03:P PF00:6 Pc10:S A111:V Sp13:L
-P01:P P11:P Pc12:S Sp10:L P02:P Qa01:V P00:P Pc11:S Sp12:L Qa11:V OF11:5 Pc03:S Sp11:L OF12:4 O11:P Pc02:S Sp03:L
-O12:P OF10:1 Oc11:S Sp02:L OF13:3 O10:P Oc12:S So11:L O13:P Pc00:S So12:L Oc10:S Sp00:L Oc13:S So10:L Pc01:S So13:L
-Sp01:L"""
+LOADS = """g00 g01 g11 sc0010 sc0011 adj01 sc0000 sc0001 adj00 sc1001 sc1000 sc1010 sc1011 g10 sc0100 h0 h1 sc0101 sc0110 adj10 sc0111 adj11 sc1101 sc1100 sc1111 sc1110 w"""
+ORDER = """Gc00:V Gx010:0 Gx011:1 Gd010:S Qg00:V Gd011:S Gc11:V E0010:S E0011:S Qg01:V E0012:S E0013:S Qg11:V M0011:V E0000:S
+E0001:S M0010:V E0002:S E0003:S Qp0010:V M0000:V E1002:S E1003:S M0001:V E1000:S E1001:S Qp0000:V E1010:S E1011:S
+DF001:2 M1001:V DF002:3 D001:P D002:P E1012:S E1013:S M1000:V DF003:4 DF000:5 D003:P C002:S D000:P C001:V Gx101:6
+C003:S M1011:V Gx100:7 C000:S Gd101:S T001:0 M1010:V Gd100:S Hx00:1 B001:S Qp1000:V T000:3 E0100:S E0101:S Hd00:V
+Hx01:2 Qg10:V B000:S Hx10:4 A001:V Hd01:S DF102:5 Qp1010:V DF103:6 E0102:S E0103:S DF100:7 Qb00:V D100:P E0110:S
+E0111:S Qh0:V D103:P M0100:V PF01:0 C100:S DF101:1 D102:P E0112:S E0113:S M0101:V PF02:3 D101:P C101:S A000:V C103:S
+Qp0100:V T100:2 E1102:S E1103:S M0110:V Hx11:7 B100:S DF011:1 M0111:V DF010:6 E1100:S E1101:S DF013:2 C102:V E1112:S
+E1113:S Qp0110:V DF012:5 Hd10:V E1110:S E1111:S D012:P M1100:V D011:P D010:P D013:P C011:S T101:4 M1101:V C013:S
+W01:1 C012:S W00:2 M1111:V C010:S T011:5 Wc01:S Qp1100:V W11:6 B101:S M1110:V Wc00:S DF112:1 Hd11:S T010:4 Qp1111:V
+B011:S W10:2 Qw0:V B010:S DF110:7 Qp1110:V DF113:5 Wc11:S Qh1:V DF111:4 A100:S D113:P Qb01:V D111:P D110:P A101:V
+PF00:6 Wc10:S D112:P Qa00:V P01:P C111:S P02:P C110:V PF03:2 C113:S P00:P Qa10:V P03:P C112:S OF03:4 Qw1:V Pc03:S
+T110:7 Pc00:V Pc02:S T111:5 Sp03:L Qb10:V Pc01:S OF02:1 Sp00:L A011:V B110:S OF00:2 Sp01:L O03:P A110:V B111:S
+O00:P Sp02:L O02:P Oc03:S PF12:6 Qb11:V OF01:3 Oc00:S PF13:0 So03:L A010:V O01:P Oc02:S P13:P So00:L A111:V Oc01:S
+PF11:7 So02:L P12:P Pc13:S Qa01:V PF10:5 So01:L P11:P Pc12:S Qa11:V P10:P Sp13:L OF12:4 OF13:2 Sp12:L Pc10:S OF10:1
+O13:P Pc11:S O12:P Sp10:L Oc13:S OF11:3 Sp11:L O10:P Oc12:S O11:P So13:L Oc10:S So12:L Oc11:S So10:L So11:L"""
 
 
 def tile_gatlayer_pa_v_kernel(tc, q, k, h, w_v, adj, scores, lse, grad_out, out_0, out_1):
@@ -107,7 +107,7 @@ def tile_gatlayer_pa_v_kernel(tc, q, k, h, w_v, adj, scores, lse, grad_out, out_
                 if ld[:2] == "sc":
                     n, G, g, hf = [int(x) for x in ld[2:]]
                     key = "sc%d%d%d" % (n, G, g)
-                    if hf == 0:
+                    if key not in T:
                         sb(key, [P, 4, 512], F32, "sc", 5)
                     nc.sync.dma_start(out=T[key][:, 2 * hf : 2 * hf + 2, :], in_=scores_v[n, g][:, 2 * hf : 2 * hf + 2, 512 * G : 512 * G + 512])
                 elif ld[:3] == "adj":
@@ -131,6 +131,17 @@ def tile_gatlayer_pa_v_kernel(tc, q, k, h, w_v, adj, scores, lse, grad_out, out_
                     words = T[src][:, 2 * kk + i, :].bitcast(F32)
                     for u in range(2):
                         nc.tensor.transpose(bk[:, 128 * (2 * i + u) : 128 * (2 * i + u) + 128], words[:, col0 + u : col0 + 256 : 2], ident[:])
+
+            identb = pool.tile([P, P], BF16, name="identb", tag="identb")
+            make_identity(nc, identb[:])
+
+            def spread(key, b, src):
+                T[key] = psum.tile([P, 1024], BF16, name="bank%d" % b, tag="bank%d" % b, bufs=1)
+                for q in range(2):
+                    nc.tensor.matmul(T[key][:, 512 * q : 512 * q + 512].rearrange("p (c s) -> p c s", s=4), lhsT=identb[:], rhs=src(q), start=True, stop=True)
+
+            def spread_out(eng, dst, kk, key):
+                copy(eng, T[dst][:, 256 * kk : 256 * kk + 256, :].rearrange("p c s -> p (c s)"), T[key][:])
 
             def words_out(eng, dst, kk, bk):
                 copy(
@@ -176,6 +187,27 @@ def tile_gatlayer_pa_v_kernel(tc, q, k, h, w_v, adj, scores, lse, grad_out, out_
                     n, g = d
                     grouped("gg%d%d" % (n, g), "gg", 3)
                     copy(e, T["gg%d%d" % (n, g)][:].rearrange("p (t m) s -> p t m s", t=4), T["g%d%d" % (n, g)][:].rearrange("p s (m t) -> p t m s", t=4))
+                elif kind == "Gx":
+                    n, g, kk = d
+                    src = T["g%d%d" % (n, g)]
+                    spread(nm, int(e), lambda q: src[:].rearrange("p s (m t) -> p t m s", t=4)[:, 2 * kk + q])
+                elif kind == "Gd":
+                    n, g, kk = d
+                    if "gg%d%d" % (n, g) not in T:
+                        grouped("gg%d%d" % (n, g), "gg", 3)
+                    spread_out(e, "gg%d%d" % (n, g), kk, "Gx" + nm[2:])
+                elif kind == "Hx":
+                    src = T["h%d" % d[0]]
+                    kk = d[1]
+                    spread(nm, int(e), lambda q: src[:, :, 256 * kk + 128 * q : 256 * kk + 128 * q + 128].rearrange("p s c -> p c s"))
+                elif kind == "Hd":
+                    if "hh%d" % d[0] not in T:
+                        grouped("hh%d" % d[0], "hh", 1)
+                    spread_out(e, "hh%d" % d[0], d[1], "Hx" + nm[2:])
+                elif kind == "Ax":
+                    src = T["v%d%d" % (d[0], d[1])]
+                    kk = d[2]
+                    spread(nm, int(e), lambda q: src[:, :, 256 * kk + 128 * q : 256 * kk + 128 * q + 128].rearrange("p s c -> p c s"))
                 elif kind == "Qg":
                     key = "gg%d%d" % (d[0], d[1])
                     codes(key, "g", 4)
@@ -216,6 +248,9 @@ def tile_gatlayer_pa_v_kernel(tc, q, k, h, w_v, adj, scores, lse, grad_out, out_
                     if key not in T:
                         grouped(key, "a", 2)
                     c = slice(256 * hh, 256 * hh + 256)
+                    if "Ax" + nm[1:] in T:
+                        spread_out(e, key, hh, "Ax" + nm[1:])
+                        continue
                     copy(e, T[key][:, c, :].rearrange("p (c i) t -> p c t i", i=4), T["v%d%d" % (n, G)][:, :, c].rearrange("p t (c i) -> p c t i", i=4))
                 elif kind == "Qa" or kind == "Qb":
                     key = kind[1] + "%d%d" % (d[0], d[1])

from contextlib import ExitStack

import concourse.mybir as mybir
from concourse.masks import make_identity

F32 = mybir.dt.float32
BF16 = mybir.dt.bfloat16
U32 = mybir.dt.uint32
U8 = mybir.dt.uint8
E4M3 = mybir.dt.float8_e4m3fn_x4
E5M2 = mybir.dt.float8_e5m2_x4
EXP = mybir.ActivationFunctionType.Exp
MULT = mybir.AluOpType.mult

FLOPS = 2 * 1024 * 1024 * 1024 * 2
BYTES = 18890752

P = 128
LOADS = """g00 g01 g11 sc0010 sc0011 adj01 sc0000 sc0001 adj00 sc1001 sc1000 sc1010 sc1011 g10 sc0100 h0 h1 sc0101 sc0110 adj10 sc0111 adj11 sc1101 sc1100 sc1111 sc1110 w"""
ORDER = """Gc00:V Gx010:0 Gx011:1 Gd010:S Qg00:V Gd011:S Gc11:V E0010:S E0011:S Qg01:V E0012:S E0013:S Qg11:V M0011:V E0000:S
E0001:S M0010:V E0002:S E0003:S Qp0010:V M0000:V E1002:S E1003:S M0001:V E1000:S E1001:S Qp0000:V E1010:S E1011:S
DF001:2 M1001:V DF002:3 D001:P D002:P E1012:S E1013:S M1000:V DF003:4 DF000:5 D003:P C002:S D000:P C001:V Gx101:6
C003:S M1011:V Gx100:7 C000:S Gd101:S T001:0 M1010:V Gd100:S Hx00:1 B001:S Qp1000:V T000:3 E0100:S E0101:S Hd00:V
Hx01:2 Qg10:V B000:S Hx10:4 A001:V Hd01:S DF102:5 Qp1010:V DF103:6 E0102:S E0103:S DF100:7 Qb00:V D100:P E0110:S
E0111:S Qh0:V D103:P M0100:V PF01:0 C100:S DF101:1 D102:P E0112:S E0113:S M0101:V PF02:3 D101:P C101:S A000:V C103:S
Qp0100:V T100:2 E1102:S E1103:S M0110:V Hx11:7 B100:S DF011:1 M0111:V DF010:6 E1100:S E1101:S DF013:2 C102:V E1112:S
E1113:S Qp0110:V DF012:5 Hd10:V E1110:S E1111:S D012:P M1100:V D011:P D010:P D013:P C011:S T101:4 M1101:V C013:S
W01:1 C012:S W00:2 M1111:V C010:S T011:5 Wc01:S Qp1100:V W11:6 B101:S M1110:V Wc00:S DF112:1 Hd11:S T010:4 Qp1111:V
B011:S W10:2 Qw0:V B010:S DF110:7 Qp1110:V DF113:5 Wc11:S Qh1:V DF111:4 A100:S D113:P Qb01:V D111:P D110:P A101:V
PF00:6 Wc10:S D112:P Qa00:V P01:P C111:S P02:P C110:V PF03:2 C113:S P00:P Qa10:V P03:P C112:S OF03:4 Qw1:V Pc03:S
T110:7 Pc00:V Pc02:S T111:5 Sp03:L Qb10:V Pc01:S OF02:1 Sp00:L A011:V B110:S OF00:2 Sp01:L O03:P A110:V B111:S
O00:P Sp02:L O02:P Oc03:S PF12:6 Qb11:V OF01:3 Oc00:S PF13:0 So03:L A010:V O01:P Oc02:S P13:P So00:L A111:V Oc01:S
PF11:7 So02:L P12:P Pc13:S Qa01:V PF10:5 So01:L P11:P Pc12:S Qa11:V P10:P Sp13:L OF12:4 OF13:2 Sp12:L Pc10:S OF10:1
O13:P Pc11:S O12:P Sp10:L Oc13:S OF11:3 Sp11:L O10:P Oc12:S O11:P So13:L Oc10:S So12:L Oc11:S So10:L So11:L"""


def tile_gatlayer_pa_v_kernel(tc, q, k, h, w_v, adj, scores, lse, grad_out, out_0, out_1):
    nc = tc.nc
    with ExitStack() as ctx:
        pool = ctx.enter_context(tc.tile_pool(name="sb", bufs=1))
        psum = ctx.enter_context(tc.psum_pool(name="ps", bufs=1))

        scores_v = scores[0].rearrange("n (g p s) j -> n g p s j", p=P, s=4)
        adj_v = adj.rearrange("(g p s) j -> g p s j", p=P, s=4)
        g_v = grad_out[0].rearrange("(g p s) f -> g p s f", p=P, s=4)
        h_v = h[0].rearrange("(g p s) c -> g p s c", p=P, s=4)
        w_vv = w_v.rearrange("(a p) f -> p a f", p=P)
        out0_v = out_0[0].rearrange("(a p) c -> a p c", p=P)
        out1_v = out_1.rearrange("(a p) f -> a p f", p=P)

        T = {}

        def sb(key, shape, dt, tag, bufs):
            T[key] = pool.tile(shape, dt, name=tag, tag=tag, bufs=bufs, align_bytes=64)
            return T[key]

        def grouped(key, tag, bufs):
            return sb(key, [P, 512, 4], BF16, tag, bufs)

        def codes(key, tag, bufs):
            sb("c" + key, [P, 512], U32, "c" + tag, bufs)
            sb("s" + key, [P, 512], U8, "s" + tag, bufs)

        def quant(key, src, fmt, lo=0, hi=512):
            nc.vector.quantize_mx(
                out=T["c" + key][:, lo:hi].bitcast(fmt),
                scales=T["s" + key][:, lo:hi],
                in_=T[src][:, lo:hi, :].rearrange("p c t -> p (c t)"),
            )

        def mm(bank, lk, lf, cols, rk, rf, start, stop):
            nc.tensor.matmul_mx(
                out=bank[:],
                lhsT=T["c" + lk][:, cols].bitcast(lf),
                lhsT_scale=T["s" + lk][:, cols],
                rhs=T["c" + rk][:].bitcast(rf),
                rhs_scale=T["s" + rk][:],
                start=start,
                stop=stop,
            )

        def copy(eng, out, in_):
            if eng == "V":
                nc.vector.tensor_copy(out=out, in_=in_)
            else:
                nc.scalar.copy(out=out, in_=in_)

        def bank(key, b):
            T[key] = psum.tile([P, 512], F32, name="bank%d" % b, tag="bank%d" % b, bufs=1)
            return T[key]

        def blk(j):
            return slice(128 * j, 128 * j + 128)

        with tc.manual_schedule():
            dummy = pool.tile([P, 1], F32, name="dummy", tag="dummy")
            nc.vector.memset(dummy[:], 0.0)
            warm = pool.tile([P, 1], F32, name="warm", tag="warm")
            nc.scalar.activation(warm[:], dummy[:], EXP)
            ident = pool.tile([P, P], F32, name="ident", tag="ident")
            make_identity(nc, ident[:])
            lse_sb = pool.tile([P, 4, 4], F32, name="lse_sb", tag="lse_sb")
            nlse = pool.tile([P, 4, 4], F32, name="nlse", tag="nlse")
            nc.scalar.dma_start(out=lse_sb[:], in_=lse.rearrange("b n i -> (b n i)").rearrange("(q p s) -> p q s", p=P, s=4))

            for ld in LOADS.split():
                if ld[:2] == "sc":
                    n, G, g, hf = [int(x) for x in ld[2:]]
                    key = "sc%d%d%d" % (n, G, g)
                    if key not in T:
                        sb(key, [P, 4, 512], F32, "sc", 5)
                    nc.sync.dma_start(out=T[key][:, 2 * hf : 2 * hf + 2, :], in_=scores_v[n, g][:, 2 * hf : 2 * hf + 2, 512 * G : 512 * G + 512])
                elif ld[:3] == "adj":
                    G, g = int(ld[3]), int(ld[4])
                    sb(ld, [P, 4, 512], BF16, "adj", 4)
                    nc.sync.dma_start(out=T[ld][:], in_=adj_v[g][:, :, 512 * G : 512 * G + 512])
                elif ld[0] == "g":
                    n, g = int(ld[1]), int(ld[2])
                    sb(ld, [P, 4, 512], BF16, "raw", 4)
                    nc.sync.dma_start(out=T[ld][:], in_=g_v[g][:, :, 512 * n : 512 * n + 512])
                elif ld[0] == "h":
                    sb(ld, [P, 4, 512], BF16, "raw", 4)
                    nc.sync.dma_start(out=T[ld][:], in_=h_v[int(ld[1])])
                elif ld == "w":
                    sb(ld, [P, 4, 1024], BF16, "w", 1)
                    nc.sync.dma_start(out=T[ld][:], in_=w_vv)
            nc.vector.tensor_scalar(out=nlse[:], in0=lse_sb[:], scalar1=-1.0, scalar2=None, op0=MULT)

            def transposes(src, col0, kk, bk):
                for i in range(2):
                    words = T[src][:, 2 * kk + i, :].bitcast(F32)
                    for u in range(2):
                        nc.tensor.transpose(bk[:, 128 * (2 * i + u) : 128 * (2 * i + u) + 128], words[:, col0 + u : col0 + 256 : 2], ident[:])

            identb = pool.tile([P, P], BF16, name="identb", tag="identb")
            make_identity(nc, identb[:])

            def spread(key, b, src):
                T[key] = psum.tile([P, 1024], BF16, name="bank%d" % b, tag="bank%d" % b, bufs=1)
                for q in range(2):
                    nc.tensor.matmul(T[key][:, 512 * q : 512 * q + 512].rearrange("p (c s) -> p c s", s=4), lhsT=identb[:], rhs=src(q), start=True, stop=True)

            def spread_out(eng, dst, kk, key):
                copy(eng, T[dst][:, 256 * kk : 256 * kk + 256, :].rearrange("p c s -> p (c s)"), T[key][:])

            def words_out(eng, dst, kk, bk):
                copy(
                    eng,
                    T[dst][:].rearrange("p c t -> p (c t)").bitcast(F32)[:, 512 * kk : 512 * kk + 512].rearrange("p (i r u) -> p i r u", i=2, u=2),
                    bk[:].rearrange("p (i u r) -> p i r u", i=2, u=2),
                )

            for item in ORDER.split():
                nm, e = item.split(":")
                kind = nm
                for dg in "0123456789":
                    kind = kind.replace(dg, "")
                d = [int(x) for x in nm[len(kind) :]]
                if kind == "E":
                    n, G, g, s = d
                    key = "e%d%d%d" % (n, G, g)
                    if key not in T:
                        sb(key, [P, 4, 512], F32, "e", 3)
                    nc.scalar.activation(T[key][:, s, :], T["sc%d%d%d" % (n, G, g)][:, s, :], EXP, bias=nlse[:, 2 * n + g, s : s + 1])
                elif kind == "M":
                    n, G, g, hh = d
                    key = "p%d%d%d" % (n, G, g)
                    if key not in T:
                        grouped(key, "gp", 3)
                    c = slice(256 * hh, 256 * hh + 256)
                    nc.vector.tensor_tensor(
                        out=T[key][:, c, :].rearrange("p (c i) s -> p c s i", i=4),
                        in0=T["e%d%d%d" % (n, G, g)][:, :, c].rearrange("p s (c i) -> p c s i", i=4),
                        in1=T["adj%d%d" % (G, g)][:, :, c].rearrange("p s (c i) -> p c s i", i=4),
                        op=MULT,
                    )
                elif kind == "Qp":
                    n, G, g, hh = d
                    key = "p%d%d%d" % (n, G, g)
                    if "c" + key not in T:
                        codes(key, "p", 6)
                    if (n, G, g) == (1, 1, 1):
                        quant(key, key, E4M3, 256 * hh, 256 * hh + 256)
                    else:
                        quant(key, key, E4M3)
                elif kind == "Gc":
                    n, g = d
                    grouped("gg%d%d" % (n, g), "gg", 3)
                    copy(e, T["gg%d%d" % (n, g)][:].rearrange("p (t m) s -> p t m s", t=4), T["g%d%d" % (n, g)][:].rearrange("p s (m t) -> p t m s", t=4))
                elif kind == "Gx":
                    n, g, kk = d
                    src = T["g%d%d" % (n, g)]
                    spread(nm, int(e), lambda q: src[:].rearrange("p s (m t) -> p t m s", t=4)[:, 2 * kk + q])
                elif kind == "Gd":
                    n, g, kk = d
                    if "gg%d%d" % (n, g) not in T:
                        grouped("gg%d%d" % (n, g), "gg", 3)
                    spread_out(e, "gg%d%d" % (n, g), kk, "Gx" + nm[2:])
                elif kind == "Hx":
                    src = T["h%d" % d[0]]
                    kk = d[1]
                    spread(nm, int(e), lambda q: src[:, :, 256 * kk + 128 * q : 256 * kk + 128 * q + 128].rearrange("p s c -> p c s"))
                elif kind == "Hd":
                    if "hh%d" % d[0] not in T:
                        grouped("hh%d" % d[0], "hh", 1)
                    spread_out(e, "hh%d" % d[0], d[1], "Hx" + nm[2:])
                elif kind == "Ax":
                    src = T["v%d%d" % (d[0], d[1])]
                    kk = d[2]
                    spread(nm, int(e), lambda q: src[:, :, 256 * kk + 128 * q : 256 * kk + 128 * q + 128].rearrange("p s c -> p c s"))
                elif kind == "Qg":
                    key = "gg%d%d" % (d[0], d[1])
                    codes(key, "g", 4)
                    quant(key, key, E5M2)
                elif kind == "Hc":
                    grouped("hh%d" % d[0], "hh", 1)
                    copy(e, T["hh%d" % d[0]][:].rearrange("p (c i) s -> p c s i", i=4), T["h%d" % d[0]][:].rearrange("p s (c i) -> p c s i", i=4))
                elif kind == "Qh":
                    key = "hh%d" % d[0]
                    codes(key, "h", 2)
                    quant(key, key, E4M3)
                elif kind == "W":
                    transposes("w", 256 * d[0], d[1], bank(nm, int(e)))
                elif kind == "Wc":
                    key = "ww%d" % d[0]
                    if key not in T:
                        grouped(key, "ww", 1)
                    words_out(e, key, d[1], T["W%d%d" % (d[0], d[1])])
                elif kind == "Qw":
                    key = "ww%d" % d[0]
                    codes(key, "w", 2)
                    quant(key, key, E4M3)
                elif kind == "DF":
                    n, G, t = d
                    mm(bank("D%d%d%d" % (n, G, t), int(e)), "gg%d0" % n, E5M2, blk(t), "p%d%d0" % (n, G), E4M3, True, False)
                elif kind == "D":
                    n, G, t = d
                    mm(T[nm], "gg%d1" % n, E5M2, blk(t), "p%d%d1" % (n, G), E4M3, False, True)
                elif kind == "C":
                    n, G, t = d
                    key = "v%d%d" % (n, G)
                    if key not in T:
                        sb(key, [P, 4, 512], BF16, "v", 2)
                    copy(e, T[key][:, t, :], T["D%d%d%d" % (n, G, t)][:])
                elif kind == "A":
                    n, G, hh = d
                    key = "a%d%d" % (n, G)
                    if key not in T:
                        grouped(key, "a", 2)
                    c = slice(256 * hh, 256 * hh + 256)
                    if "Ax" + nm[1:] in T:
                        spread_out(e, key, hh, "Ax" + nm[1:])
                        continue
                    copy(e, T[key][:, c, :].rearrange("p (c i) t -> p c t i", i=4), T["v%d%d" % (n, G)][:, :, c].rearrange("p t (c i) -> p c t i", i=4))
                elif kind == "Qa" or kind == "Qb":
                    key = kind[1] + "%d%d" % (d[0], d[1])
                    codes(key, kind[1], 4)
                    quant(key, key, E5M2)
                elif kind == "T":
                    transposes("v%d%d" % (d[0], d[1]), 0, d[2], bank(nm, int(e)))
                elif kind == "B":
                    n, G, kk = d
                    key = "b%d%d" % (n, G)
                    if key not in T:
                        grouped(key, "b", 2)
                    words_out(e, key, kk, T["T%d%d%d" % (n, G, kk)])
                elif kind == "OF":
                    G, j = d
                    mm(bank("O%d%d" % (G, j), int(e)), "a0%d" % G, E5M2, blk(j), "ww0", E4M3, True, False)
                elif kind == "O":
                    G, j = d
                    mm(T[nm], "a1%d" % G, E5M2, blk(j), "ww1", E4M3, False, True)
                elif kind == "PF":
                    n, j = d
                    mm(bank("P%d%d" % (n, j), int(e)), "hh0", E4M3, blk(j), "b%d0" % n, E5M2, True, False)
                elif kind == "P":
                    n, j = d
                    mm(T[nm], "hh1", E4M3, blk(j), "b%d1" % n, E5M2, False, True)
                elif kind == "Oc":
                    o = sb("o" + nm, [P, 512], F32, "o", 6)
                    copy(e, o[:], T["O%d%d" % (d[0], d[1])][:])
                elif kind == "Pc":
                    o = sb("o" + nm, [P, 512], F32, "o", 6)
                    copy(e, o[:].rearrange("p (m t) -> p m t", t=4), T["P%d%d" % (d[0], d[1])][:].rearrange("p (t m) -> p m t", t=4))
                elif kind == "So":
                    nc.sync.dma_start(out=out0_v[4 * d[0] + d[1]], in_=T["oOc%d%d" % (d[0], d[1])][:])
                elif kind == "Sp":
                    nc.sync.dma_start(out=out1_v[d[1]][:, 512 * d[0] : 512 * d[0] + 512], in_=T["oPc%d%d" % (d[0], d[1])][:])
